import numpy as np
import ml_dtypes


def mxq(x, axis, fmt="e4m3"):
    dtype, down = {"e4m3": (ml_dtypes.float8_e4m3fn, 7), "e5m2": (ml_dtypes.float8_e5m2, 14)}[fmt]
    v = np.moveaxis(np.asarray(x, np.float32).astype(ml_dtypes.bfloat16).astype(np.float64), axis, -1)
    blocks = v.reshape(v.shape[:-1] + (-1, 32))
    amax = np.abs(blocks).max(-1, keepdims=True)
    byte = np.maximum(np.where(amax > 0, np.frexp(amax)[1] - 1 + 127, 0) - down, 1)
    scale = np.exp2(byte - 127.0)
    codes = (blocks / scale).astype(np.float32).astype(dtype).astype(np.float64)
    return np.moveaxis((codes * scale).reshape(v.shape), -1, axis)


WIDE = False


def mx_kscale(k):
    if not WIDE:
        return np.ones(k)
    levels = np.array([10, -10, 5, -5, 0])
    a = np.random.permutation(np.resize(levels, k // 512 * 4)).reshape(k // 512, 4)
    idx = np.arange(k)
    return np.exp2(a[idx // 512, idx % 128 // 32])


BF16 = ml_dtypes.bfloat16


def bf(x):
    return np.asarray(x, np.float32).astype(BF16)


def f64(x):
    return np.asarray(x).astype(np.float64)


B, C, T, P, N, D = 2, 8, 1024, 128, 4, 512
L = T // P
G = L // N


def gelu_tanh(v):
    return 0.5 * v * (1.0 + np.tanh(np.sqrt(2.0 / np.pi) * (v + 0.044715 * v**3)))


def setup_inputs():
    s = mx_kscale(D)
    return {'x': bf(np.random.standard_normal((B, C, T))),
            'emb_W': bf(np.random.standard_normal((P, D)) / np.sqrt(P) * s),
            'emb_b': bf(np.random.standard_normal(D) * 0.2 * s),
            'enc_W1': bf(np.random.standard_normal((N, D, D)) / np.sqrt(D) / s[None, :, None]),
            'enc_b1': bf(np.random.standard_normal((N, D)) * 0.2),
            'enc_W2': bf(np.random.standard_normal((N, D, D)) / np.sqrt(D)),
            'enc_b2': bf(np.random.standard_normal((N, D)) * 0.2)}


def reference(x, emb_W, emb_b, enc_W1, enc_b1, enc_W2, enc_b2):
    e = f64(x).reshape(B * C * L, P) @ f64(emb_W) + f64(emb_b)
    e = np.moveaxis(e.reshape(B, C, G, N, D), 3, 0).reshape(N, B * C * G, D)
    a = (mxq(e, 2, 'e4m3') @ mxq(f64(enc_W1), 1, 'e4m3')) + f64(enc_b1)[:, None, :]
    g = gelu_tanh(a)
    o = (mxq(g, 2, 'e4m3') @ mxq(f64(enc_W2), 1, 'e4m3')) + f64(enc_b2)[:, None, :]
    return o.reshape(N, B, C, G, D)

@@ -1,0 +1,168 @@
+from contextlib import ExitStack
+
+import concourse.mybir as mybir
+from concourse.masks import make_identity
+
+BF16 = mybir.dt.bfloat16
+F32 = mybir.dt.float32
+U32 = mybir.dt.uint32
+U8 = mybir.dt.uint8
+FP8X4 = mybir.dt.float8_e4m3fn_x4
+ADD = mybir.AluOpType.add
+GELU = mybir.ActivationFunctionType.Gelu_apprx_tanh
+
+P = 128
+PACK = 4
+MODELS = 4
+WIDTH = 512
+ROWS = 32
+RUN = 4
+VECTOR_COLS = 256
+
+FLOPS = 2 * P * P * WIDTH + 2 * (2 * P * WIDTH * WIDTH)
+
+
+def regroup(copy, grouped, raw, cols):
+    copy(
+        out=grouped[:, cols, :].rearrange("p (c i) t -> p c t i", i=RUN),
+        in_=raw[:, :, cols].rearrange("p t (c i) -> p c t i", i=RUN),
+    )
+
+
+def tile_model_pa_s_kernel(tc, x, emb_W, emb_b, enc_W1, enc_b1, enc_W2, enc_b2, out):
+    nc = tc.nc
+    with ExitStack() as ctx:
+        keep = ctx.enter_context(tc.tile_pool(name="keep", bufs=1))
+        work = ctx.enter_context(tc.tile_pool(name="work", bufs=2))
+        psum = ctx.enter_context(tc.psum_pool(name="psum", bufs=1))
+        psum_a = ctx.enter_context(tc.psum_pool(name="psum_a", bufs=2))
+
+        w_views = [enc_W1[n].rearrange("(p t) h -> p t h", t=PACK) for n in range(MODELS)]
+        w_views += [enc_W2[n].rearrange("(t p) f -> p t f", p=P) for n in range(MODELS)]
+        w_raw = []
+        for c in range(2 * MODELS):
+            raw = keep.tile([P, PACK, WIDTH], BF16, name="w_raw_%d" % c)
+            nc.sync.dma_start(out=raw[:], in_=w_views[c])
+            w_raw.append(raw)
+
+        ident = keep.tile([P, P], BF16)
+        make_identity(nc, ident[:])
+
+        x_sb = keep.tile([P, P], BF16)
+        nc.scalar.dma_start(out=x_sb[:], in_=x.rearrange("b c (j s) -> (b c j) s", s=P))
+        emb_w_sb = keep.tile([P, WIDTH], BF16)
+        nc.scalar.dma_start(out=emb_w_sb[:], in_=emb_W)
+        emb_b_sb = keep.tile([P, PACK], BF16)
+        nc.scalar.dma_start(out=emb_b_sb[:], in_=emb_b.rearrange("(p t) -> p t", t=PACK))
+        b1_rows = keep.tile([P, P], BF16)
+        nc.vector.memset(b1_rows[:], 0.0)
+        nc.scalar.dma_start(
+            out=b1_rows[0 : MODELS * PACK, :],
+            in_=enc_b1.rearrange("n (t p) -> (n t) p", p=P),
+        )
+        b2_rows = keep.tile([P, WIDTH], BF16)
+        for n in range(MODELS):
+            nc.gpsimd.dma_start(
+                out=b2_rows[n * ROWS : (n + 1) * ROWS, :],
+                in_=enc_b2[n].partition_broadcast(ROWS),
+            )
+
+        warm = keep.tile([P, 1], F32)
+        nc.vector.memset(warm[:], 0.0)
+        nc.scalar.activation(out=warm[:], in_=warm[:], func=GELU)
+
+        g_masked = keep.tile([P, MODELS, P, PACK], BF16, align_bytes=64)
+        nc.vector.memset(g_masked[:], 0.0)
+
+        xT_ps = psum.tile([P, P], BF16)
+        nc.tensor.transpose(xT_ps[:], x_sb[:], ident[:])
+        xT_sb = keep.tile([P, MODELS, ROWS], BF16)
+        nc.scalar.copy(out=xT_sb[:], in_=xT_ps[:].rearrange("p (i n) -> p n i", n=MODELS))
+
+        b1T_ps = psum.tile([P, P], BF16)
+        nc.tensor.transpose(b1T_ps[:], b1_rows[:], ident[:])
+        b1T_sb = keep.tile([P, MODELS * PACK], BF16)
+        nc.scalar.copy(out=b1T_sb[:], in_=b1T_ps[:, 0 : MODELS * PACK])
+
+        e_ps = psum.tile([P, PACK, P], F32)
+        emb_w_by_t = emb_w_sb[:].rearrange("s (p t) -> s t p", t=PACK)
+        for t in range(PACK):
+            nc.tensor.matmul(
+                out=e_ps[:, t, :],
+                lhsT=emb_w_by_t[:, t, :],
+                rhs=xT_sb[:].rearrange("s n i -> s (n i)"),
+                start=True,
+                stop=True,
+            )
+        e_grouped = keep.tile([P, P, PACK], BF16, align_bytes=64)
+        nc.vector.tensor_tensor(
+            out=e_grouped[:],
+            in0=e_ps[:].rearrange("p t r -> p r t"),
+            in1=emb_b_sb[:].unsqueeze(1).to_broadcast([P, P, PACK]),
+            op=ADD,
+        )
+        e_codes = keep.tile([P, P], U32, align_bytes=64)
+        e_scales = keep.tile([P, P], U8, align_bytes=64)
+        nc.vector.quantize_mx(
+            out=e_codes[:].bitcast(FP8X4),
+            scales=e_scales[:],
+            in_=e_grouped[:].rearrange("p r t -> p (r t)"),
+        )
+
+        g_codes = keep.tile([P, MODELS, P], U32, align_bytes=64)
+        g_scales = keep.tile([P, MODELS, P], U8, align_bytes=64)
+        o_ps = psum.tile([P, WIDTH], F32)
+
+        for c in range(2 * MODELS):
+            n = c % MODELS
+            grouped = keep.tile([P, WIDTH, PACK], BF16, name="w_grouped_%d" % c, align_bytes=64)
+            regroup(nc.vector.tensor_copy, grouped, w_raw[c], slice(0, VECTOR_COLS))
+            regroup(nc.scalar.copy, grouped, w_raw[c], slice(VECTOR_COLS, WIDTH))
+            w_codes = keep.tile([P, WIDTH], U32, name="w_codes_%d" % c, align_bytes=64)
+            w_scales = keep.tile([P, WIDTH], U8, name="w_scales_%d" % c, align_bytes=64)
+            nc.vector.quantize_mx(
+                out=w_codes[:].bitcast(FP8X4),
+                scales=w_scales[:],
+                in_=grouped[:].rearrange("p w t -> p (w t)"),
+            )
+
+            if c < MODELS:
+                a_ps = psum_a.tile([P, PACK, P], F32)
+                for t in range(PACK):
+                    nc.tensor.matmul_mx(
+                        out=a_ps[:, t, :],
+                        lhsT=w_codes[:, t * P : (t + 1) * P].bitcast(FP8X4),
+                        lhsT_scale=w_scales[:, t * P : (t + 1) * P],
+                        rhs=e_codes[:].bitcast(FP8X4),
+                        rhs_scale=e_scales[:],
+                        start=True,
+                        stop=True,
+                    )
+                own = slice(n * ROWS, (n + 1) * ROWS)
+                a_sb = work.tile([P, ROWS, PACK], F32)
+                nc.vector.tensor_tensor(
+                    out=a_sb[:],
+                    in0=a_ps[:, :, own].rearrange("p t i -> p i t"),
+                    in1=b1T_sb[:, n * PACK : (n + 1) * PACK].unsqueeze(1).to_broadcast([P, ROWS, PACK]),
+                    op=ADD,
+                )
+                nc.scalar.activation(out=g_masked[:, n, own, :], in_=a_sb[:], func=GELU)
+                nc.vector.quantize_mx(
+                    out=g_codes[:, n, :].bitcast(FP8X4),
+                    scales=g_scales[:, n, :],
+                    in_=g_masked[:, n, :, :].rearrange("p r t -> p (r t)"),
+                )
+            else:
+                nc.tensor.matmul_mx(
+                    out=o_ps[:],
+                    lhsT=g_codes[:, n, :].bitcast(FP8X4),
+                    lhsT_scale=g_scales[:, n, :],
+                    rhs=w_codes[:].bitcast(FP8X4),
+                    rhs_scale=w_scales[:],
+                    start=(n == 0),
+                    stop=(n == MODELS - 1),
+                )
+
+        o_sb = keep.tile([P, WIDTH], F32)
+        nc.vector.tensor_tensor(out=o_sb[:], in0=o_ps[:], in1=b2_rows[:], op=ADD)
+        nc.sync.dma_start(out=out.rearrange("n b c l f -> (n b c l) f"), in_=o_sb[:])

@@ -16,6 +16,7 @@ PACK = 4
 MODELS = 4
 WIDTH = 512
 ROWS = 32
+BIAS_ROWS = MODELS * PACK
 RUN = 4
 VECTOR_COLS = 256
 
@@ -37,14 +38,6 @@ def tile_model_pa_s_kernel(tc, x, emb_W, emb_b, enc_W1, enc_b1, enc_W2, enc_b2, 
         psum = ctx.enter_context(tc.psum_pool(name="psum", bufs=1))
         psum_a = ctx.enter_context(tc.psum_pool(name="psum_a", bufs=2))
 
-        w_views = [enc_W1[n].rearrange("(p t) h -> p t h", t=PACK) for n in range(MODELS)]
-        w_views += [enc_W2[n].rearrange("(t p) f -> p t f", p=P) for n in range(MODELS)]
-        w_raw = []
-        for c in range(2 * MODELS):
-            raw = keep.tile([P, PACK, WIDTH], BF16, name="w_raw_%d" % c)
-            nc.sync.dma_start(out=raw[:], in_=w_views[c])
-            w_raw.append(raw)
-
         ident = keep.tile([P, P], BF16)
         make_identity(nc, ident[:])
 
@@ -54,18 +47,23 @@ def tile_model_pa_s_kernel(tc, x, emb_W, emb_b, enc_W1, enc_b1, enc_W2, enc_b2, 
         nc.scalar.dma_start(out=emb_w_sb[:], in_=emb_W)
         emb_b_sb = keep.tile([P, PACK], BF16)
         nc.scalar.dma_start(out=emb_b_sb[:], in_=emb_b.rearrange("(p t) -> p t", t=PACK))
-        b1_rows = keep.tile([P, P], BF16)
-        nc.vector.memset(b1_rows[:], 0.0)
+        bias_rows = keep.tile([P, P], BF16)
+        nc.vector.memset(bias_rows[:], 0.0)
         nc.scalar.dma_start(
-            out=b1_rows[0 : MODELS * PACK, :],
-            in_=enc_b1.rearrange("n (t p) -> (n t) p", p=P),
+            out=bias_rows[0:BIAS_ROWS, :], in_=enc_b1.rearrange("n (t p) -> (n t) p", p=P)
         )
-        b2_rows = keep.tile([P, WIDTH], BF16)
-        for n in range(MODELS):
-            nc.gpsimd.dma_start(
-                out=b2_rows[n * ROWS : (n + 1) * ROWS, :],
-                in_=enc_b2[n].partition_broadcast(ROWS),
-            )
+        nc.scalar.dma_start(
+            out=bias_rows[BIAS_ROWS : 2 * BIAS_ROWS, :],
+            in_=enc_b2.rearrange("n (c p) -> (n c) p", p=P),
+        )
+
+        w_views = [enc_W1[n].rearrange("(p t) h -> p t h", t=PACK) for n in range(MODELS)]
+        w_views += [enc_W2[n].rearrange("(t p) f -> p t f", p=P) for n in range(MODELS)]
+        w_raw = []
+        for c in range(2 * MODELS):
+            raw = keep.tile([P, PACK, WIDTH], BF16, name="w_raw_%d" % c)
+            nc.sync.dma_start(out=raw[:], in_=w_views[c])
+            w_raw.append(raw)
 
         warm = keep.tile([P, 1], F32)
         nc.vector.memset(warm[:], 0.0)
@@ -79,11 +77,10 @@ def tile_model_pa_s_kernel(tc, x, emb_W, emb_b, enc_W1, enc_b1, enc_W2, enc_b2, 
         xT_sb = keep.tile([P, MODELS, ROWS], BF16)
         nc.scalar.copy(out=xT_sb[:], in_=xT_ps[:].rearrange("p (i n) -> p n i", n=MODELS))
 
-        b1T_ps = psum.tile([P, P], BF16)
-        nc.tensor.transpose(b1T_ps[:], b1_rows[:], ident[:])
-        b1T_sb = keep.tile([P, MODELS * PACK], BF16)
-        nc.scalar.copy(out=b1T_sb[:], in_=b1T_ps[:, 0 : MODELS * PACK])
-
+        biasT_ps = psum.tile([P, P], BF16)
+        nc.tensor.transpose(biasT_ps[:], bias_rows[:], ident[:])
+        b1T_sb = keep.tile([P, BIAS_ROWS], BF16)
+        nc.scalar.copy(out=b1T_sb[:], in_=biasT_ps[:, 0:BIAS_ROWS])
         e_ps = psum.tile([P, PACK, P], F32)
         emb_w_by_t = emb_w_sb[:].rearrange("s (p t) -> s t p", t=PACK)
         for t in range(PACK):
@@ -108,6 +105,22 @@ def tile_model_pa_s_kernel(tc, x, emb_W, emb_b, enc_W1, enc_b1, enc_W2, enc_b2, 
             scales=e_scales[:],
             in_=e_grouped[:].rearrange("p r t -> p (r t)"),
         )
+
+        b2T_wide = keep.tile([P, PACK, MODELS, ROWS], BF16)
+        nc.scalar.copy(
+            out=b2T_wide[:],
+            in_=biasT_ps[:, BIAS_ROWS : 2 * BIAS_ROWS]
+            .rearrange("p (n c) -> p c n", c=PACK)
+            .unsqueeze(3)
+            .to_broadcast([P, PACK, MODELS, ROWS]),
+        )
+        b2_ps = psum.tile([P, PACK, P], BF16)
+        for c in range(PACK):
+            nc.tensor.transpose(
+                b2_ps[:, c, :], b2T_wide[:, c, :, :].rearrange("p n i -> p (n i)"), ident[:]
+            )
+        b2_rows = keep.tile([P, WIDTH], BF16)
+        nc.scalar.copy(out=b2_rows[:], in_=b2_ps[:].rearrange("p c f -> p (c f)"))
 
         g_codes = keep.tile([P, MODELS, P], U32, align_bytes=64)
         g_scales = keep.tile([P, MODELS, P], U8, align_bytes=64)

@@ -14,25 +14,20 @@ GELU = mybir.ActivationFunctionType.Gelu_apprx_tanh
 P = 128
 PACK = 4
 MODELS = 4
+WEIGHTS = 2 * MODELS
 WIDTH = 512
+HALF = 256
 ROWS = 32
 BIAS_ROWS = MODELS * PACK
 RUN = 4
-VECTOR_COLS = 256
 
 FLOPS = 2 * P * P * WIDTH + 2 * (2 * P * WIDTH * WIDTH)
-
-
-def regroup(copy, grouped, raw, cols):
-    copy(
-        out=grouped[:, cols, :].rearrange("p (c i) t -> p c t i", i=RUN),
-        in_=raw[:, :, cols].rearrange("p t (c i) -> p c t i", i=RUN),
-    )
 
 
 def tile_model_pa_s_kernel(tc, x, emb_W, emb_b, enc_W1, enc_b1, enc_W2, enc_b2, out):
     nc = tc.nc
     with ExitStack() as ctx:
+        ctx.enter_context(tc.manual_schedule())
         keep = ctx.enter_context(tc.tile_pool(name="keep", bufs=1))
         work = ctx.enter_context(tc.tile_pool(name="work", bufs=2))
         psum = ctx.enter_context(tc.psum_pool(name="psum", bufs=1))
@@ -40,47 +35,59 @@ def tile_model_pa_s_kernel(tc, x, emb_W, emb_b, enc_W1, enc_b1, enc_W2, enc_b2, 
 
         ident = keep.tile([P, P], BF16)
         make_identity(nc, ident[:])
-
-        x_sb = keep.tile([P, P], BF16)
-        nc.scalar.dma_start(out=x_sb[:], in_=x.rearrange("b c (j s) -> (b c j) s", s=P))
-        emb_w_sb = keep.tile([P, WIDTH], BF16)
-        nc.scalar.dma_start(out=emb_w_sb[:], in_=emb_W)
-        emb_b_sb = keep.tile([P, PACK], BF16)
-        nc.scalar.dma_start(out=emb_b_sb[:], in_=emb_b.rearrange("(p t) -> p t", t=PACK))
         bias_rows = keep.tile([P, P], BF16)
         nc.vector.memset(bias_rows[:], 0.0)
-        nc.scalar.dma_start(
-            out=bias_rows[0:BIAS_ROWS, :], in_=enc_b1.rearrange("n (t p) -> (n t) p", p=P)
-        )
-        nc.scalar.dma_start(
-            out=bias_rows[BIAS_ROWS : 2 * BIAS_ROWS, :],
-            in_=enc_b2.rearrange("n (c p) -> (n c) p", p=P),
-        )
+        warm = keep.tile([P, 1], F32)
+        nc.vector.memset(warm[:], 0.0)
+        g_masked = keep.tile([P, MODELS, P, PACK], BF16, align_bytes=64)
+        nc.vector.memset(g_masked[:], 0.0)
 
+        x_sb = keep.tile([P, P], BF16)
+        nc.sync.dma_start(out=x_sb[:], in_=x.rearrange("b c (j s) -> (b c j) s", s=P))
+        emb_w_sb = keep.tile([P, WIDTH], BF16)
+        nc.sync.dma_start(out=emb_w_sb[:], in_=emb_W)
+        emb_b_sb = keep.tile([P, PACK], BF16)
+        nc.sync.dma_start(out=emb_b_sb[:], in_=emb_b.rearrange("(p t) -> p t", t=PACK))
         w_views = [enc_W1[n].rearrange("(p t) h -> p t h", t=PACK) for n in range(MODELS)]
         w_views += [enc_W2[n].rearrange("(t p) f -> p t f", p=P) for n in range(MODELS)]
         w_raw = []
-        for c in range(2 * MODELS):
-            raw = keep.tile([P, PACK, WIDTH], BF16, name="w_raw_%d" % c)
-            nc.sync.dma_start(out=raw[:], in_=w_views[c])
-            w_raw.append(raw)
-
-        warm = keep.tile([P, 1], F32)
-        nc.vector.memset(warm[:], 0.0)
+        w_grouped = []
+        w_codes = []
+        w_scales = []
+        for c in range(WEIGHTS):
+            w_raw.append(keep.tile([P, PACK, WIDTH], BF16, name="w_raw_%d" % c))
+            nc.sync.dma_start(out=w_raw[c][:], in_=w_views[c])
+            if c == 0:
+                nc.sync.dma_start(
+                    out=bias_rows[0:BIAS_ROWS, :],
+                    in_=enc_b1.rearrange("n (t p) -> (n t) p", p=P),
+                )
+                nc.sync.dma_start(
+                    out=bias_rows[BIAS_ROWS : 2 * BIAS_ROWS, :],
+                    in_=enc_b2.rearrange("n (c p) -> (n c) p", p=P),
+                )
+            w_grouped.append(
+                keep.tile([P, WIDTH, PACK], BF16, name="w_grouped_%d" % c, align_bytes=64)
+            )
+            w_codes.append(keep.tile([P, WIDTH], U32, name="w_codes_%d" % c, align_bytes=64))
+            w_scales.append(keep.tile([P, WIDTH], U8, name="w_scales_%d" % c, align_bytes=64))
         nc.scalar.activation(out=warm[:], in_=warm[:], func=GELU)
+        halves = [slice(0, HALF), slice(HALF, WIDTH)]
 
-        g_masked = keep.tile([P, MODELS, P, PACK], BF16, align_bytes=64)
-        nc.vector.memset(g_masked[:], 0.0)
+        def regroup(c):
+            for copy, cols in zip([nc.vector.tensor_copy, nc.scalar.copy], halves):
+                copy(
+                    out=w_grouped[c][:, cols, :].rearrange("p (c i) t -> p c t i", i=RUN),
+                    in_=w_raw[c][:, :, cols].rearrange("p t (c i) -> p c t i", i=RUN),
+                )
 
         xT_ps = psum.tile([P, P], BF16)
         nc.tensor.transpose(xT_ps[:], x_sb[:], ident[:])
         xT_sb = keep.tile([P, MODELS, ROWS], BF16)
         nc.scalar.copy(out=xT_sb[:], in_=xT_ps[:].rearrange("p (i n) -> p n i", n=MODELS))
 
-        biasT_ps = psum.tile([P, P], BF16)
-        nc.tensor.transpose(biasT_ps[:], bias_rows[:], ident[:])
-        b1T_sb = keep.tile([P, BIAS_ROWS], BF16)
-        nc.scalar.copy(out=b1T_sb[:], in_=biasT_ps[:, 0:BIAS_ROWS])
+        regroup(0)
+
         e_ps = psum.tile([P, PACK, P], F32)
         emb_w_by_t = emb_w_sb[:].rearrange("s (p t) -> s t p", t=PACK)
         for t in range(PACK):
@@ -106,6 +113,10 @@ def tile_model_pa_s_kernel(tc, x, emb_W, emb_b, enc_W1, enc_b1, enc_W2, enc_b2, 
             in_=e_grouped[:].rearrange("p r t -> p (r t)"),
         )
 
+        biasT_ps = psum.tile([P, P], BF16)
+        nc.tensor.transpose(biasT_ps[:], bias_rows[:], ident[:])
+        b1T_sb = keep.tile([P, BIAS_ROWS], BF16)
+        nc.scalar.copy(out=b1T_sb[:], in_=biasT_ps[:, 0:BIAS_ROWS])
         b2T_wide = keep.tile([P, PACK, MODELS, ROWS], BF16)
         nc.scalar.copy(
             out=b2T_wide[:],
@@ -122,60 +133,82 @@ def tile_model_pa_s_kernel(tc, x, emb_W, emb_b, enc_W1, enc_b1, enc_W2, enc_b2, 
         b2_rows = keep.tile([P, WIDTH], BF16)
         nc.scalar.copy(out=b2_rows[:], in_=b2_ps[:].rearrange("p c f -> p (c f)"))
 
+        a_ps = [None] * MODELS
+        a_sb = [None] * MODELS
         g_codes = keep.tile([P, MODELS, P], U32, align_bytes=64)
         g_scales = keep.tile([P, MODELS, P], U8, align_bytes=64)
-        o_ps = psum.tile([P, WIDTH], F32)
+        o_ps = [psum.tile([P, HALF], F32, name="o_ps_%d" % h) for h in range(2)]
 
-        for c in range(2 * MODELS):
+        def quantise_and_multiply(c, h):
             n = c % MODELS
-            grouped = keep.tile([P, WIDTH, PACK], BF16, name="w_grouped_%d" % c, align_bytes=64)
-            regroup(nc.vector.tensor_copy, grouped, w_raw[c], slice(0, VECTOR_COLS))
-            regroup(nc.scalar.copy, grouped, w_raw[c], slice(VECTOR_COLS, WIDTH))
-            w_codes = keep.tile([P, WIDTH], U32, name="w_codes_%d" % c, align_bytes=64)
-            w_scales = keep.tile([P, WIDTH], U8, name="w_scales_%d" % c, align_bytes=64)
             nc.vector.quantize_mx(
-                out=w_codes[:].bitcast(FP8X4),
-                scales=w_scales[:],
-                in_=grouped[:].rearrange("p w t -> p (w t)"),
+                out=w_codes[c][:, halves[h]].bitcast(FP8X4),
+                scales=w_scales[c][:, halves[h]],
+                in_=w_grouped[c][:, halves[h], :].rearrange("p w t -> p (w t)"),
             )
-
             if c < MODELS:
-                a_ps = psum_a.tile([P, PACK, P], F32)
-                for t in range(PACK):
+                if h == 0:
+                    a_ps[n] = psum_a.tile([P, PACK, P], F32, name="a_ps")
+                for t in range(2 * h, 2 * h + 2):
                     nc.tensor.matmul_mx(
-                        out=a_ps[:, t, :],
-                        lhsT=w_codes[:, t * P : (t + 1) * P].bitcast(FP8X4),
-                        lhsT_scale=w_scales[:, t * P : (t + 1) * P],
+                        out=a_ps[n][:, t, :],
+                        lhsT=w_codes[c][:, t * P : (t + 1) * P].bitcast(FP8X4),
+                        lhsT_scale=w_scales[c][:, t * P : (t + 1) * P],
                         rhs=e_codes[:].bitcast(FP8X4),
                         rhs_scale=e_scales[:],
                         start=True,
                         stop=True,
                     )
-                own = slice(n * ROWS, (n + 1) * ROWS)
-                a_sb = work.tile([P, ROWS, PACK], F32)
-                nc.vector.tensor_tensor(
-                    out=a_sb[:],
-                    in0=a_ps[:, :, own].rearrange("p t i -> p i t"),
-                    in1=b1T_sb[:, n * PACK : (n + 1) * PACK].unsqueeze(1).to_broadcast([P, ROWS, PACK]),
-                    op=ADD,
-                )
-                nc.scalar.activation(out=g_masked[:, n, own, :], in_=a_sb[:], func=GELU)
-                nc.vector.quantize_mx(
-                    out=g_codes[:, n, :].bitcast(FP8X4),
-                    scales=g_scales[:, n, :],
-                    in_=g_masked[:, n, :, :].rearrange("p r t -> p (r t)"),
-                )
             else:
                 nc.tensor.matmul_mx(
-                    out=o_ps[:],
+                    out=o_ps[h][:],
                     lhsT=g_codes[:, n, :].bitcast(FP8X4),
                     lhsT_scale=g_scales[:, n, :],
-                    rhs=w_codes[:].bitcast(FP8X4),
-                    rhs_scale=w_scales[:],
+                    rhs=w_codes[c][:, halves[h]].bitcast(FP8X4),
+                    rhs_scale=w_scales[c][:, halves[h]],
                     start=(n == 0),
                     stop=(n == MODELS - 1),
                 )
 
+        def add_b1(n):
+            own = slice(n * ROWS, (n + 1) * ROWS)
+            a_sb[n] = work.tile([P, ROWS, PACK], F32, name="a_sb")
+            nc.vector.tensor_tensor(
+                out=a_sb[n][:],
+                in0=a_ps[n][:, :, own].rearrange("p t i -> p i t"),
+                in1=b1T_sb[:, n * PACK : (n + 1) * PACK].unsqueeze(1).to_broadcast([P, ROWS, PACK]),
+                op=ADD,
+            )
+
+        def gelu(n):
+            own = slice(n * ROWS, (n + 1) * ROWS)
+            nc.scalar.activation(out=g_masked[:, n, own, :], in_=a_sb[n][:], func=GELU)
+
+        def quantise_g(n):
+            nc.vector.quantize_mx(
+                out=g_codes[:, n, :].bitcast(FP8X4),
+                scales=g_scales[:, n, :],
+                in_=g_masked[:, n, :, :].rearrange("p r t -> p (r t)"),
+            )
+
+        for s in range(WEIGHTS + 1):
+            if 0 <= s - 4 < MODELS:
+                quantise_g(s - 4)
+            if 0 <= s - 3 < MODELS:
+                gelu(s - 3)
+            if s >= 1:
+                quantise_and_multiply(s - 1, 1)
+            if s < WEIGHTS:
+                quantise_and_multiply(s, 0)
+            if 0 <= s - 2 < MODELS:
+                add_b1(s - 2)
+            if s + 1 < WEIGHTS:
+                regroup(s + 1)
+
         o_sb = keep.tile([P, WIDTH], F32)
-        nc.vector.tensor_tensor(out=o_sb[:], in0=o_ps[:], in1=b2_rows[:], op=ADD)
-        nc.sync.dma_start(out=out.rearrange("n b c l f -> (n b c l) f"), in_=o_sb[:])
+        out_rows = out.rearrange("n b c l f -> (n b c l) f")
+        for h in range(2):
+            nc.vector.tensor_tensor(
+                out=o_sb[:, halves[h]], in0=o_ps[h][:], in1=b2_rows[:, halves[h]], op=ADD
+            )
+            nc.sync.dma_start(out=out_rows[:, halves[h]], in_=o_sb[:, halves[h]])

@@ -20,6 +20,7 @@ HALF = 256
 ROWS = 32
 BIAS_ROWS = MODELS * PACK
 RUN = 4
+VECTOR_COLS = 224
 
 FLOPS = 2 * P * P * WIDTH + 2 * (2 * P * WIDTH * WIDTH)
 
@@ -48,6 +49,13 @@ def tile_model_pa_s_kernel(tc, x, emb_W, emb_b, enc_W1, enc_b1, enc_W2, enc_b2, 
         nc.sync.dma_start(out=emb_w_sb[:], in_=emb_W)
         emb_b_sb = keep.tile([P, PACK], BF16)
         nc.sync.dma_start(out=emb_b_sb[:], in_=emb_b.rearrange("(p t) -> p t", t=PACK))
+        nc.sync.dma_start(
+            out=bias_rows[0:BIAS_ROWS, :], in_=enc_b1.rearrange("n (t p) -> (n t) p", p=P)
+        )
+        nc.sync.dma_start(
+            out=bias_rows[BIAS_ROWS : 2 * BIAS_ROWS, :],
+            in_=enc_b2.rearrange("n (c p) -> (n c) p", p=P),
+        )
         w_views = [enc_W1[n].rearrange("(p t) h -> p t h", t=PACK) for n in range(MODELS)]
         w_views += [enc_W2[n].rearrange("(t p) f -> p t f", p=P) for n in range(MODELS)]
         w_raw = []
@@ -57,15 +65,6 @@ def tile_model_pa_s_kernel(tc, x, emb_W, emb_b, enc_W1, enc_b1, enc_W2, enc_b2, 
         for c in range(WEIGHTS):
             w_raw.append(keep.tile([P, PACK, WIDTH], BF16, name="w_raw_%d" % c))
             nc.sync.dma_start(out=w_raw[c][:], in_=w_views[c])
-            if c == 0:
-                nc.sync.dma_start(
-                    out=bias_rows[0:BIAS_ROWS, :],
-                    in_=enc_b1.rearrange("n (t p) -> (n t) p", p=P),
-                )
-                nc.sync.dma_start(
-                    out=bias_rows[BIAS_ROWS : 2 * BIAS_ROWS, :],
-                    in_=enc_b2.rearrange("n (c p) -> (n c) p", p=P),
-                )
             w_grouped.append(
                 keep.tile([P, WIDTH, PACK], BF16, name="w_grouped_%d" % c, align_bytes=64)
             )
@@ -75,7 +74,8 @@ def tile_model_pa_s_kernel(tc, x, emb_W, emb_b, enc_W1, enc_b1, enc_W2, enc_b2, 
         halves = [slice(0, HALF), slice(HALF, WIDTH)]
 
         def regroup(c):
-            for copy, cols in zip([nc.vector.tensor_copy, nc.scalar.copy], halves):
+            shares = [slice(0, VECTOR_COLS), slice(VECTOR_COLS, WIDTH)]
+            for copy, cols in zip([nc.vector.tensor_copy, nc.scalar.copy], shares):
                 copy(
                     out=w_grouped[c][:, cols, :].rearrange("p (c i) t -> p c t i", i=RUN),
                     in_=w_raw[c][:, :, cols].rearrange("p t (c i) -> p c t i", i=RUN),
@@ -85,6 +85,19 @@ def tile_model_pa_s_kernel(tc, x, emb_W, emb_b, enc_W1, enc_b1, enc_W2, enc_b2, 
         nc.tensor.transpose(xT_ps[:], x_sb[:], ident[:])
         xT_sb = keep.tile([P, MODELS, ROWS], BF16)
         nc.scalar.copy(out=xT_sb[:], in_=xT_ps[:].rearrange("p (i n) -> p n i", n=MODELS))
+
+        biasT_ps = psum.tile([P, P], BF16)
+        nc.tensor.transpose(biasT_ps[:], bias_rows[:], ident[:])
+        b1T_sb = keep.tile([P, BIAS_ROWS], BF16)
+        nc.scalar.copy(out=b1T_sb[:], in_=biasT_ps[:, 0:BIAS_ROWS])
+        b2T_wide = keep.tile([P, PACK, MODELS, ROWS], BF16)
+        nc.scalar.copy(
+            out=b2T_wide[:],
+            in_=biasT_ps[:, BIAS_ROWS : 2 * BIAS_ROWS]
+            .rearrange("p (n c) -> p c n", c=PACK)
+            .unsqueeze(3)
+            .to_broadcast([P, PACK, MODELS, ROWS]),
+        )
 
         regroup(0)
 
@@ -113,18 +126,6 @@ def tile_model_pa_s_kernel(tc, x, emb_W, emb_b, enc_W1, enc_b1, enc_W2, enc_b2, 
             in_=e_grouped[:].rearrange("p r t -> p (r t)"),
         )
 
-        biasT_ps = psum.tile([P, P], BF16)
-        nc.tensor.transpose(biasT_ps[:], bias_rows[:], ident[:])
-        b1T_sb = keep.tile([P, BIAS_ROWS], BF16)
-        nc.scalar.copy(out=b1T_sb[:], in_=biasT_ps[:, 0:BIAS_ROWS])
-        b2T_wide = keep.tile([P, PACK, MODELS, ROWS], BF16)
-        nc.scalar.copy(
-            out=b2T_wide[:],
-            in_=biasT_ps[:, BIAS_ROWS : 2 * BIAS_ROWS]
-            .rearrange("p (n c) -> p c n", c=PACK)
-            .unsqueeze(3)
-            .to_broadcast([P, PACK, MODELS, ROWS]),
-        )
         b2_ps = psum.tile([P, PACK, P], BF16)
         for c in range(PACK):
             nc.tensor.transpose(

@@ -18,9 +18,10 @@ WEIGHTS = 2 * MODELS
 WIDTH = 512
 HALF = 256
 ROWS = 32
+WINDOW = 2 * ROWS
 BIAS_ROWS = MODELS * PACK
 RUN = 4
-VECTOR_COLS = 224
+VECTOR_COLS = [224] * (WEIGHTS - 1) + [HALF]
 
 FLOPS = 2 * P * P * WIDTH + 2 * (2 * P * WIDTH * WIDTH)
 
@@ -40,9 +41,30 @@ def tile_model_pa_s_kernel(tc, x, emb_W, emb_b, enc_W1, enc_b1, enc_W2, enc_b2, 
         nc.vector.memset(bias_rows[:], 0.0)
         warm = keep.tile([P, 1], F32)
         nc.vector.memset(warm[:], 0.0)
-        g_masked = keep.tile([P, MODELS, P, PACK], BF16, align_bytes=64)
-        nc.vector.memset(g_masked[:], 0.0)
+        g_window = keep.tile([P, MODELS, WINDOW, PACK], BF16, align_bytes=64)
+        nc.vector.memset(g_window[:], 0.0)
+        g_codes = keep.tile([P, MODELS, P], U32, align_bytes=64)
+        nc.gpsimd.memset(g_codes[:], 0)
+        g_scales = keep.tile([P, MODELS, P], U8, align_bytes=64)
+        nc.gpsimd.memset(g_scales[:], 0)
 
+        w_views = [enc_W1[n].rearrange("(p t) h -> p t h", t=PACK) for n in range(MODELS)]
+        w_views += [enc_W2[n].rearrange("(t p) f -> p t f", p=P) for n in range(MODELS)]
+        w_raw = []
+        w_grouped = []
+        w_codes = []
+        w_scales = []
+
+        def load_weight(c):
+            w_raw.append(keep.tile([P, PACK, WIDTH], BF16, name="w_raw_%d" % c))
+            nc.sync.dma_start(out=w_raw[c][:], in_=w_views[c])
+            w_grouped.append(
+                keep.tile([P, WIDTH, PACK], BF16, name="w_grouped_%d" % c, align_bytes=64)
+            )
+            w_codes.append(keep.tile([P, WIDTH], U32, name="w_codes_%d" % c, align_bytes=64))
+            w_scales.append(keep.tile([P, WIDTH], U8, name="w_scales_%d" % c, align_bytes=64))
+
+        load_weight(0)
         x_sb = keep.tile([P, P], BF16)
         nc.sync.dma_start(out=x_sb[:], in_=x.rearrange("b c (j s) -> (b c j) s", s=P))
         emb_w_sb = keep.tile([P, WIDTH], BF16)
@@ -56,35 +78,25 @@ def tile_model_pa_s_kernel(tc, x, emb_W, emb_b, enc_W1, enc_b1, enc_W2, enc_b2, 
             out=bias_rows[BIAS_ROWS : 2 * BIAS_ROWS, :],
             in_=enc_b2.rearrange("n (c p) -> (n c) p", p=P),
         )
-        w_views = [enc_W1[n].rearrange("(p t) h -> p t h", t=PACK) for n in range(MODELS)]
-        w_views += [enc_W2[n].rearrange("(t p) f -> p t f", p=P) for n in range(MODELS)]
-        w_raw = []
-        w_grouped = []
-        w_codes = []
-        w_scales = []
-        for c in range(WEIGHTS):
-            w_raw.append(keep.tile([P, PACK, WIDTH], BF16, name="w_raw_%d" % c))
-            nc.sync.dma_start(out=w_raw[c][:], in_=w_views[c])
-            w_grouped.append(
-                keep.tile([P, WIDTH, PACK], BF16, name="w_grouped_%d" % c, align_bytes=64)
-            )
-            w_codes.append(keep.tile([P, WIDTH], U32, name="w_codes_%d" % c, align_bytes=64))
-            w_scales.append(keep.tile([P, WIDTH], U8, name="w_scales_%d" % c, align_bytes=64))
+        for c in range(1, WEIGHTS):
+            load_weight(c)
         nc.scalar.activation(out=warm[:], in_=warm[:], func=GELU)
         halves = [slice(0, HALF), slice(HALF, WIDTH)]
 
         def regroup(c):
-            shares = [slice(0, VECTOR_COLS), slice(VECTOR_COLS, WIDTH)]
+            shares = [slice(0, VECTOR_COLS[c]), slice(VECTOR_COLS[c], WIDTH)]
             for copy, cols in zip([nc.vector.tensor_copy, nc.scalar.copy], shares):
                 copy(
                     out=w_grouped[c][:, cols, :].rearrange("p (c i) t -> p c t i", i=RUN),
                     in_=w_raw[c][:, :, cols].rearrange("p t (c i) -> p c t i", i=RUN),
                 )
 
+        regroup(0)
+
         xT_ps = psum.tile([P, P], BF16)
         nc.tensor.transpose(xT_ps[:], x_sb[:], ident[:])
         xT_sb = keep.tile([P, MODELS, ROWS], BF16)
-        nc.scalar.copy(out=xT_sb[:], in_=xT_ps[:].rearrange("p (i n) -> p n i", n=MODELS))
+        nc.vector.tensor_copy(out=xT_sb[:], in_=xT_ps[:].rearrange("p (i n) -> p n i", n=MODELS))
 
         biasT_ps = psum.tile([P, P], BF16)
         nc.tensor.transpose(biasT_ps[:], bias_rows[:], ident[:])
@@ -99,8 +111,6 @@ def tile_model_pa_s_kernel(tc, x, emb_W, emb_b, enc_W1, enc_b1, enc_W2, enc_b2, 
             .to_broadcast([P, PACK, MODELS, ROWS]),
         )
 
-        regroup(0)
-
         e_ps = psum.tile([P, PACK, P], F32)
         emb_w_by_t = emb_w_sb[:].rearrange("s (p t) -> s t p", t=PACK)
         for t in range(PACK):
@@ -112,41 +122,28 @@ def tile_model_pa_s_kernel(tc, x, emb_W, emb_b, enc_W1, enc_b1, enc_W2, enc_b2, 
                 stop=True,
             )
         e_grouped = keep.tile([P, P, PACK], BF16, align_bytes=64)
-        nc.vector.tensor_tensor(
-            out=e_grouped[:],
-            in0=e_ps[:].rearrange("p t r -> p r t"),
-            in1=emb_b_sb[:].unsqueeze(1).to_broadcast([P, P, PACK]),
-            op=ADD,
-        )
         e_codes = keep.tile([P, P], U32, align_bytes=64)
         e_scales = keep.tile([P, P], U8, align_bytes=64)
-        nc.vector.quantize_mx(
-            out=e_codes[:].bitcast(FP8X4),
-            scales=e_scales[:],
-            in_=e_grouped[:].rearrange("p r t -> p (r t)"),
-        )
 
         b2_ps = psum.tile([P, PACK, P], BF16)
         for c in range(PACK):
             nc.tensor.transpose(
                 b2_ps[:, c, :], b2T_wide[:, c, :, :].rearrange("p n i -> p (n i)"), ident[:]
             )
-        b2_rows = keep.tile([P, WIDTH], BF16)
-        nc.scalar.copy(out=b2_rows[:], in_=b2_ps[:].rearrange("p c f -> p (c f)"))
 
         a_ps = [None] * MODELS
         a_sb = [None] * MODELS
-        g_codes = keep.tile([P, MODELS, P], U32, align_bytes=64)
-        g_scales = keep.tile([P, MODELS, P], U8, align_bytes=64)
         o_ps = [psum.tile([P, HALF], F32, name="o_ps_%d" % h) for h in range(2)]
 
-        def quantise_and_multiply(c, h):
-            n = c % MODELS
+        def quantise(c, cols):
             nc.vector.quantize_mx(
-                out=w_codes[c][:, halves[h]].bitcast(FP8X4),
-                scales=w_scales[c][:, halves[h]],
-                in_=w_grouped[c][:, halves[h], :].rearrange("p w t -> p (w t)"),
+                out=w_codes[c][:, cols].bitcast(FP8X4),
+                scales=w_scales[c][:, cols],
+                in_=w_grouped[c][:, cols, :].rearrange("p w t -> p (w t)"),
             )
+
+        def multiply(c, h):
+            n = c % MODELS
             if c < MODELS:
                 if h == 0:
                     a_ps[n] = psum_a.tile([P, PACK, P], F32, name="a_ps")
@@ -182,29 +179,53 @@ def tile_model_pa_s_kernel(tc, x, emb_W, emb_b, enc_W1, enc_b1, enc_W2, enc_b2, 
             )
 
         def gelu(n):
-            own = slice(n * ROWS, (n + 1) * ROWS)
-            nc.scalar.activation(out=g_masked[:, n, own, :], in_=a_sb[n][:], func=GELU)
+            own = slice(n % 2 * ROWS, (n % 2 + 1) * ROWS)
+            nc.scalar.activation(out=g_window[:, n, own, :], in_=a_sb[n][:], func=GELU)
 
         def quantise_g(n):
+            pair = slice(n // 2 * WINDOW, (n // 2 + 1) * WINDOW)
             nc.vector.quantize_mx(
-                out=g_codes[:, n, :].bitcast(FP8X4),
-                scales=g_scales[:, n, :],
-                in_=g_masked[:, n, :, :].rearrange("p r t -> p (r t)"),
+                out=g_codes[:, n, pair].bitcast(FP8X4),
+                scales=g_scales[:, n, pair],
+                in_=g_window[:, n, :, :].rearrange("p r t -> p (r t)"),
             )
 
-        for s in range(WEIGHTS + 1):
+        quantise(0, halves[0])
+        nc.vector.tensor_tensor(
+            out=e_grouped[:],
+            in0=e_ps[:].rearrange("p t r -> p r t"),
+            in1=emb_b_sb[:].unsqueeze(1).to_broadcast([P, P, PACK]),
+            op=ADD,
+        )
+        quantise(0, halves[1])
+        regroup(1)
+        nc.vector.quantize_mx(
+            out=e_codes[:].bitcast(FP8X4),
+            scales=e_scales[:],
+            in_=e_grouped[:].rearrange("p r t -> p (r t)"),
+        )
+        multiply(0, 0)
+        multiply(0, 1)
+        b2_rows = keep.tile([P, WIDTH], BF16)
+        nc.scalar.copy(out=b2_rows[:], in_=b2_ps[:].rearrange("p c f -> p (c f)"))
+
+        for s in range(1, WEIGHTS):
             if 0 <= s - 4 < MODELS:
                 quantise_g(s - 4)
             if 0 <= s - 3 < MODELS:
                 gelu(s - 3)
-            if s >= 1:
-                quantise_and_multiply(s - 1, 1)
-            if s < WEIGHTS:
-                quantise_and_multiply(s, 0)
+            if 2 <= s < WEIGHTS:
+                quantise(s - 1, slice(0, WIDTH))
+                multiply(s - 1, 0)
+                multiply(s - 1, 1)
             if 0 <= s - 2 < MODELS:
                 add_b1(s - 2)
             if s + 1 < WEIGHTS:
                 regroup(s + 1)
+
+        for h in range(2):
+            quantise(WEIGHTS - 1, halves[h])
+            multiply(WEIGHTS - 1, h)
 
         o_sb = keep.tile([P, WIDTH], F32)
         out_rows = out.rearrange("n b c l f -> (n b c l) f")

@@ -21,7 +21,7 @@ ROWS = 32
 WINDOW = 2 * ROWS
 BIAS_ROWS = MODELS * PACK
 RUN = 4
-VECTOR_COLS = [224] * (WEIGHTS - 1) + [HALF]
+VECTOR_COLS = [HALF] + [216] * (WEIGHTS - 2) + [HALF]
 
 FLOPS = 2 * P * P * WIDTH + 2 * (2 * P * WIDTH * WIDTH)
 
@@ -206,8 +206,6 @@ def tile_model_pa_s_kernel(tc, x, emb_W, emb_b, enc_W1, enc_b1, enc_W2, enc_b2, 
         )
         multiply(0, 0)
         multiply(0, 1)
-        b2_rows = keep.tile([P, WIDTH], BF16)
-        nc.scalar.copy(out=b2_rows[:], in_=b2_ps[:].rearrange("p c f -> p (c f)"))
 
         for s in range(1, WEIGHTS):
             if 0 <= s - 4 < MODELS:
@@ -226,6 +224,9 @@ def tile_model_pa_s_kernel(tc, x, emb_W, emb_b, enc_W1, enc_b1, enc_W2, enc_b2, 
         for h in range(2):
             quantise(WEIGHTS - 1, halves[h])
             multiply(WEIGHTS - 1, h)
+
+        b2_rows = keep.tile([P, WIDTH], BF16)
+        nc.scalar.copy(out=b2_rows[:], in_=b2_ps[:].rearrange("p c f -> p (c f)"))
 
         o_sb = keep.tile([P, WIDTH], F32)
         out_rows = out.rearrange("n b c l f -> (n b c l) f")

@@ -21,7 +21,7 @@ ROWS = 32
 WINDOW = 2 * ROWS
 BIAS_ROWS = MODELS * PACK
 RUN = 4
-VECTOR_COLS = [HALF] + [216] * (WEIGHTS - 2) + [HALF]
+VECTOR_COLS = [HALF] + [240] * (WEIGHTS - 2) + [HALF]
 
 FLOPS = 2 * P * P * WIDTH + 2 * (2 * P * WIDTH * WIDTH)
 
@@ -212,7 +212,7 @@ def tile_model_pa_s_kernel(tc, x, emb_W, emb_b, enc_W1, enc_b1, enc_W2, enc_b2, 
                 quantise_g(s - 4)
             if 0 <= s - 3 < MODELS:
                 gelu(s - 3)
-            if 2 <= s < WEIGHTS:
+            if 2 <= s < WEIGHTS - 1:
                 quantise(s - 1, slice(0, WIDTH))
                 multiply(s - 1, 0)
                 multiply(s - 1, 1)
@@ -222,8 +222,9 @@ def tile_model_pa_s_kernel(tc, x, emb_W, emb_b, enc_W1, enc_b1, enc_W2, enc_b2, 
                 regroup(s + 1)
 
         for h in range(2):
-            quantise(WEIGHTS - 1, halves[h])
-            multiply(WEIGHTS - 1, h)
+            for c in range(WEIGHTS - 2, WEIGHTS):
+                quantise(c, halves[h])
+                multiply(c, h)
 
         b2_rows = keep.tile([P, WIDTH], BF16)
         nc.scalar.copy(out=b2_rows[:], in_=b2_ps[:].rearrange("p c f -> p (c f)"))

@@ -14,6 +14,7 @@ GELU = mybir.ActivationFunctionType.Gelu_apprx_tanh
 P = 128
 PACK = 4
 MODELS = 4
+ORDER = [0, 2, 1, 3]
 WEIGHTS = 2 * MODELS
 WIDTH = 512
 HALF = 256
@@ -21,7 +22,7 @@ ROWS = 32
 WINDOW = 2 * ROWS
 BIAS_ROWS = MODELS * PACK
 RUN = 4
-VECTOR_COLS = [HALF] + [240] * (WEIGHTS - 2) + [HALF]
+VECTOR_COLS = [320] + [232] * (WEIGHTS - 2) + [HALF]
 
 FLOPS = 2 * P * P * WIDTH + 2 * (2 * P * WIDTH * WIDTH)
 
@@ -37,19 +38,21 @@ def tile_model_pa_s_kernel(tc, x, emb_W, emb_b, enc_W1, enc_b1, enc_W2, enc_b2, 
 
         ident = keep.tile([P, P], BF16)
         make_identity(nc, ident[:])
-        bias_rows = keep.tile([P, P], BF16)
-        nc.vector.memset(bias_rows[:], 0.0)
+        b1_rows = keep.tile([P, P], BF16)
+        nc.vector.memset(b1_rows[:], 0.0)
+        b2_in = keep.tile([P, P], BF16)
+        nc.vector.memset(b2_in[:], 0.0)
         warm = keep.tile([P, 1], F32)
         nc.vector.memset(warm[:], 0.0)
-        g_window = keep.tile([P, MODELS, WINDOW, PACK], BF16, align_bytes=64)
+        g_window = keep.tile([P, 2, 2, WINDOW, PACK], BF16, align_bytes=64)
         nc.vector.memset(g_window[:], 0.0)
-        g_codes = keep.tile([P, MODELS, P], U32, align_bytes=64)
+        g_codes = keep.tile([P, 2, 2 * P], U32, align_bytes=64)
         nc.gpsimd.memset(g_codes[:], 0)
-        g_scales = keep.tile([P, MODELS, P], U8, align_bytes=64)
+        g_scales = keep.tile([P, 2, 2 * P], U8, align_bytes=64)
         nc.gpsimd.memset(g_scales[:], 0)
 
-        w_views = [enc_W1[n].rearrange("(p t) h -> p t h", t=PACK) for n in range(MODELS)]
-        w_views += [enc_W2[n].rearrange("(t p) f -> p t f", p=P) for n in range(MODELS)]
+        w_views = [enc_W1[n].rearrange("(p t) h -> p t h", t=PACK) for n in ORDER]
+        w_views += [enc_W2[n].rearrange("(t p) f -> p t f", p=P) for n in ORDER]
         w_raw = []
         w_grouped = []
         w_codes = []
@@ -71,41 +74,45 @@ def tile_model_pa_s_kernel(tc, x, emb_W, emb_b, enc_W1, enc_b1, enc_W2, enc_b2, 
         nc.sync.dma_start(out=emb_w_sb[:], in_=emb_W)
         emb_b_sb = keep.tile([P, PACK], BF16)
         nc.sync.dma_start(out=emb_b_sb[:], in_=emb_b.rearrange("(p t) -> p t", t=PACK))
-        nc.sync.dma_start(
-            out=bias_rows[0:BIAS_ROWS, :], in_=enc_b1.rearrange("n (t p) -> (n t) p", p=P)
-        )
-        nc.sync.dma_start(
-            out=bias_rows[BIAS_ROWS : 2 * BIAS_ROWS, :],
-            in_=enc_b2.rearrange("n (c p) -> (n c) p", p=P),
-        )
-        for c in range(1, WEIGHTS):
+        nc.sync.dma_start(out=b2_in[0:BIAS_ROWS, :], in_=enc_b2.rearrange("n (c p) -> (n c) p", p=P))
+        load_weight(1)
+        for w in range(2):
+            nc.sync.dma_start(
+                out=b1_rows[w * BIAS_ROWS // 2 : (w + 1) * BIAS_ROWS // 2, :],
+                in_=enc_b1[2 - 2 * w : 4 - 2 * w].rearrange("n (t p) -> (n t) p", p=P),
+            )
+        for c in range(2, WEIGHTS):
             load_weight(c)
         nc.scalar.activation(out=warm[:], in_=warm[:], func=GELU)
         halves = [slice(0, HALF), slice(HALF, WIDTH)]
 
-        def regroup(c):
-            shares = [slice(0, VECTOR_COLS[c]), slice(VECTOR_COLS[c], WIDTH)]
-            for copy, cols in zip([nc.vector.tensor_copy, nc.scalar.copy], shares):
-                copy(
-                    out=w_grouped[c][:, cols, :].rearrange("p (c i) t -> p c t i", i=RUN),
-                    in_=w_raw[c][:, :, cols].rearrange("p t (c i) -> p c t i", i=RUN),
-                )
+        def regroup(c, copy, first, last):
+            cols = slice(first, last)
+            copy(
+                out=w_grouped[c][:, cols, :].rearrange("p (c i) t -> p c t i", i=RUN),
+                in_=w_raw[c][:, :, cols].rearrange("p t (c i) -> p c t i", i=RUN),
+            )
 
-        regroup(0)
+        def share_regrouping(c):
+            regroup(c, nc.vector.tensor_copy, 0, VECTOR_COLS[c])
+            regroup(c, nc.scalar.copy, VECTOR_COLS[c], WIDTH)
+
+        regroup(0, nc.vector.tensor_copy, 0, HALF)
+        regroup(0, nc.scalar.copy, VECTOR_COLS[0], WIDTH)
 
         xT_ps = psum.tile([P, P], BF16)
         nc.tensor.transpose(xT_ps[:], x_sb[:], ident[:])
         xT_sb = keep.tile([P, MODELS, ROWS], BF16)
         nc.vector.tensor_copy(out=xT_sb[:], in_=xT_ps[:].rearrange("p (i n) -> p n i", n=MODELS))
 
-        biasT_ps = psum.tile([P, P], BF16)
-        nc.tensor.transpose(biasT_ps[:], bias_rows[:], ident[:])
-        b1T_sb = keep.tile([P, BIAS_ROWS], BF16)
-        nc.scalar.copy(out=b1T_sb[:], in_=biasT_ps[:, 0:BIAS_ROWS])
+        regroup(0, nc.vector.tensor_copy, HALF, VECTOR_COLS[0])
+
+        b2T_ps = psum.tile([P, P], BF16, name="biasT_ps")
+        nc.tensor.transpose(b2T_ps[:], b2_in[:], ident[:])
         b2T_wide = keep.tile([P, PACK, MODELS, ROWS], BF16)
         nc.scalar.copy(
             out=b2T_wide[:],
-            in_=biasT_ps[:, BIAS_ROWS : 2 * BIAS_ROWS]
+            in_=b2T_ps[:, 0:BIAS_ROWS]
             .rearrange("p (n c) -> p c n", c=PACK)
             .unsqueeze(3)
             .to_broadcast([P, PACK, MODELS, ROWS]),
@@ -130,9 +137,11 @@ def tile_model_pa_s_kernel(tc, x, emb_W, emb_b, enc_W1, enc_b1, enc_W2, enc_b2, 
             nc.tensor.transpose(
                 b2_ps[:, c, :], b2T_wide[:, c, :, :].rearrange("p n i -> p (n i)"), ident[:]
             )
+        b1T_ps = psum.tile([P, P], BF16, name="biasT_ps")
+        nc.tensor.transpose(b1T_ps[:], b1_rows[:], ident[:])
 
-        a_ps = [None] * MODELS
-        a_sb = [None] * MODELS
+        a_ps = [None] * 2
+        a_sb = [None] * 2
         o_ps = [psum.tile([P, HALF], F32, name="o_ps_%d" % h) for h in range(2)]
 
         def quantise(c, cols):
@@ -143,62 +152,67 @@ def tile_model_pa_s_kernel(tc, x, emb_W, emb_b, enc_W1, enc_b1, enc_W2, enc_b2, 
             )
 
         def multiply(c, h):
-            n = c % MODELS
+            n = ORDER[c % MODELS]
+            q = n % 2
+            w = 1 - n // 2
             if c < MODELS:
-                if h == 0:
-                    a_ps[n] = psum_a.tile([P, PACK, P], F32, name="a_ps")
+                if c % 2 == 0 and h == 0:
+                    a_ps[q] = psum_a.tile([P, 2, PACK, WINDOW], F32, name="a_ps")
+                patches = slice((1 - w) * WINDOW, (2 - w) * WINDOW)
                 for t in range(2 * h, 2 * h + 2):
                     nc.tensor.matmul_mx(
-                        out=a_ps[n][:, t, :],
+                        out=a_ps[q][:, w, t, :],
                         lhsT=w_codes[c][:, t * P : (t + 1) * P].bitcast(FP8X4),
                         lhsT_scale=w_scales[c][:, t * P : (t + 1) * P],
-                        rhs=e_codes[:].bitcast(FP8X4),
-                        rhs_scale=e_scales[:],
+                        rhs=e_codes[:, patches].bitcast(FP8X4),
+                        rhs_scale=e_scales[:, patches],
                         start=True,
                         stop=True,
                     )
             else:
                 nc.tensor.matmul_mx(
                     out=o_ps[h][:],
-                    lhsT=g_codes[:, n, :].bitcast(FP8X4),
-                    lhsT_scale=g_scales[:, n, :],
+                    lhsT=g_codes[:, q, w * P : (w + 1) * P].bitcast(FP8X4),
+                    lhsT_scale=g_scales[:, q, w * P : (w + 1) * P],
                     rhs=w_codes[c][:, halves[h]].bitcast(FP8X4),
                     rhs_scale=w_scales[c][:, halves[h]],
-                    start=(n == 0),
-                    stop=(n == MODELS - 1),
+                    start=(c == MODELS),
+                    stop=(c == WEIGHTS - 1),
                 )
 
-        def add_b1(n):
-            own = slice(n * ROWS, (n + 1) * ROWS)
-            a_sb[n] = work.tile([P, ROWS, PACK], F32, name="a_sb")
+        own = [slice(q * ROWS, (q + 1) * ROWS) for q in range(2)]
+        b1T_sb = keep.tile([P, BIAS_ROWS], BF16)
+        b1_by_pair = b1T_sb[:].rearrange("p (w q t) -> p q w t", w=2, q=2)
+
+        def add_b1(q):
+            a_sb[q] = work.tile([P, 2, ROWS, PACK], F32, name="a_sb")
             nc.vector.tensor_tensor(
-                out=a_sb[n][:],
-                in0=a_ps[n][:, :, own].rearrange("p t i -> p i t"),
-                in1=b1T_sb[:, n * PACK : (n + 1) * PACK].unsqueeze(1).to_broadcast([P, ROWS, PACK]),
+                out=a_sb[q][:],
+                in0=a_ps[q][:, :, :, own[q]].rearrange("p w t i -> p w i t"),
+                in1=b1_by_pair[:, q].unsqueeze(2).to_broadcast([P, 2, ROWS, PACK]),
                 op=ADD,
             )
 
-        def gelu(n):
-            own = slice(n % 2 * ROWS, (n % 2 + 1) * ROWS)
-            nc.scalar.activation(out=g_window[:, n, own, :], in_=a_sb[n][:], func=GELU)
+        def gelu(q):
+            nc.scalar.activation(out=g_window[:, q, :, own[q], :], in_=a_sb[q][:], func=GELU)
 
-        def quantise_g(n):
-            pair = slice(n // 2 * WINDOW, (n // 2 + 1) * WINDOW)
+        def quantise_g(q):
+            middle = slice(WINDOW, 3 * WINDOW)
             nc.vector.quantize_mx(
-                out=g_codes[:, n, pair].bitcast(FP8X4),
-                scales=g_scales[:, n, pair],
-                in_=g_window[:, n, :, :].rearrange("p r t -> p (r t)"),
+                out=g_codes[:, q, middle].bitcast(FP8X4),
+                scales=g_scales[:, q, middle],
+                in_=g_window[:, q].rearrange("p w j t -> p (w j t)"),
             )
 
         quantise(0, halves[0])
+        quantise(0, halves[1])
         nc.vector.tensor_tensor(
             out=e_grouped[:],
             in0=e_ps[:].rearrange("p t r -> p r t"),
             in1=emb_b_sb[:].unsqueeze(1).to_broadcast([P, P, PACK]),
             op=ADD,
         )
-        quantise(0, halves[1])
-        regroup(1)
+        share_regrouping(1)
         nc.vector.quantize_mx(
             out=e_codes[:].bitcast(FP8X4),
             scales=e_scales[:],
@@ -208,18 +222,20 @@ def tile_model_pa_s_kernel(tc, x, emb_W, emb_b, enc_W1, enc_b1, enc_W2, enc_b2, 
         multiply(0, 1)
 
         for s in range(1, WEIGHTS):
-            if 0 <= s - 4 < MODELS:
-                quantise_g(s - 4)
-            if 0 <= s - 3 < MODELS:
-                gelu(s - 3)
+            if s in (5, 7):
+                quantise_g((s - 5) // 2)
+            if s in (4, 6):
+                gelu((s - 4) // 2)
             if 2 <= s < WEIGHTS - 1:
                 quantise(s - 1, slice(0, WIDTH))
                 multiply(s - 1, 0)
                 multiply(s - 1, 1)
-            if 0 <= s - 2 < MODELS:
-                add_b1(s - 2)
+            if s in (3, 5):
+                add_b1((s - 3) // 2)
             if s + 1 < WEIGHTS:
-                regroup(s + 1)
+                share_regrouping(s + 1)
+            if s == 1:
+                nc.scalar.copy(out=b1T_sb[:], in_=b1T_ps[:, 0:BIAS_ROWS])
 
         for h in range(2):
             for c in range(WEIGHTS - 2, WEIGHTS):

from contextlib import ExitStack

import concourse.mybir as mybir
from concourse.masks import make_identity

BF16 = mybir.dt.bfloat16
F32 = mybir.dt.float32
U32 = mybir.dt.uint32
U8 = mybir.dt.uint8
FP8X4 = mybir.dt.float8_e4m3fn_x4
ADD = mybir.AluOpType.add
GELU = mybir.ActivationFunctionType.Gelu_apprx_tanh

P = 128
PACK = 4
MODELS = 4
ORDER = [0, 2, 1, 3]
WEIGHTS = 2 * MODELS
WIDTH = 512
HALF = 256
ROWS = 32
WINDOW = 2 * ROWS
BIAS_ROWS = MODELS * PACK
RUN = 4
VECTOR_COLS = [320] + [232] * (WEIGHTS - 2) + [HALF]

FLOPS = 2 * P * P * WIDTH + 2 * (2 * P * WIDTH * WIDTH)


def tile_model_pa_s_kernel(tc, x, emb_W, emb_b, enc_W1, enc_b1, enc_W2, enc_b2, out):
    nc = tc.nc
    with ExitStack() as ctx:
        ctx.enter_context(tc.manual_schedule())
        keep = ctx.enter_context(tc.tile_pool(name="keep", bufs=1))
        work = ctx.enter_context(tc.tile_pool(name="work", bufs=2))
        psum = ctx.enter_context(tc.psum_pool(name="psum", bufs=1))
        psum_a = ctx.enter_context(tc.psum_pool(name="psum_a", bufs=2))

        ident = keep.tile([P, P], BF16)
        make_identity(nc, ident[:])
        b1_rows = keep.tile([P, P], BF16)
        nc.vector.memset(b1_rows[:], 0.0)
        b2_in = keep.tile([P, P], BF16)
        nc.vector.memset(b2_in[:], 0.0)
        warm = keep.tile([P, 1], F32)
        nc.vector.memset(warm[:], 0.0)
        g_window = keep.tile([P, 2, 2, WINDOW, PACK], BF16, align_bytes=64)
        nc.vector.memset(g_window[:], 0.0)
        g_codes = keep.tile([P, 2, 2 * P], U32, align_bytes=64)
        nc.gpsimd.memset(g_codes[:], 0)
        g_scales = keep.tile([P, 2, 2 * P], U8, align_bytes=64)
        nc.gpsimd.memset(g_scales[:], 0)

        w_views = [enc_W1[n].rearrange("(p t) h -> p t h", t=PACK) for n in ORDER]
        w_views += [enc_W2[n].rearrange("(t p) f -> p t f", p=P) for n in ORDER]
        w_raw = []
        w_grouped = []
        w_codes = []
        w_scales = []

        def load_weight(c):
            w_raw.append(keep.tile([P, PACK, WIDTH], BF16, name="w_raw_%d" % c))
            nc.sync.dma_start(out=w_raw[c][:], in_=w_views[c])
            w_grouped.append(
                keep.tile([P, WIDTH, PACK], BF16, name="w_grouped_%d" % c, align_bytes=64)
            )
            w_codes.append(keep.tile([P, WIDTH], U32, name="w_codes_%d" % c, align_bytes=64))
            w_scales.append(keep.tile([P, WIDTH], U8, name="w_scales_%d" % c, align_bytes=64))

        load_weight(0)
        x_sb = keep.tile([P, P], BF16)
        nc.sync.dma_start(out=x_sb[:], in_=x.rearrange("b c (j s) -> (b c j) s", s=P))
        emb_w_sb = keep.tile([P, WIDTH], BF16)
        nc.sync.dma_start(out=emb_w_sb[:], in_=emb_W)
        emb_b_sb = keep.tile([P, PACK], BF16)
        nc.sync.dma_start(out=emb_b_sb[:], in_=emb_b.rearrange("(p t) -> p t", t=PACK))
        nc.sync.dma_start(out=b2_in[0:BIAS_ROWS, :], in_=enc_b2.rearrange("n (c p) -> (n c) p", p=P))
        load_weight(1)
        for w in range(2):
            nc.sync.dma_start(
                out=b1_rows[w * BIAS_ROWS // 2 : (w + 1) * BIAS_ROWS // 2, :],
                in_=enc_b1[2 - 2 * w : 4 - 2 * w].rearrange("n (t p) -> (n t) p", p=P),
            )
        for c in range(2, WEIGHTS):
            load_weight(c)
        nc.scalar.activation(out=warm[:], in_=warm[:], func=GELU)
        halves = [slice(0, HALF), slice(HALF, WIDTH)]

        def regroup(c, copy, first, last):
            cols = slice(first, last)
            copy(
                out=w_grouped[c][:, cols, :].rearrange("p (c i) t -> p c t i", i=RUN),
                in_=w_raw[c][:, :, cols].rearrange("p t (c i) -> p c t i", i=RUN),
            )

        def share_regrouping(c):
            regroup(c, nc.vector.tensor_copy, 0, VECTOR_COLS[c])
            regroup(c, nc.scalar.copy, VECTOR_COLS[c], WIDTH)

        regroup(0, nc.vector.tensor_copy, 0, HALF)
        regroup(0, nc.scalar.copy, VECTOR_COLS[0], WIDTH)

        xT_ps = psum.tile([P, P], BF16)
        nc.tensor.transpose(xT_ps[:], x_sb[:], ident[:])
        xT_sb = keep.tile([P, MODELS, ROWS], BF16)
        nc.vector.tensor_copy(out=xT_sb[:], in_=xT_ps[:].rearrange("p (i n) -> p n i", n=MODELS))

        regroup(0, nc.vector.tensor_copy, HALF, VECTOR_COLS[0])

        b2T_ps = psum.tile([P, P], BF16, name="biasT_ps")
        nc.tensor.transpose(b2T_ps[:], b2_in[:], ident[:])
        b2T_wide = keep.tile([P, PACK, MODELS, ROWS], BF16)
        nc.scalar.copy(
            out=b2T_wide[:],
            in_=b2T_ps[:, 0:BIAS_ROWS]
            .rearrange("p (n c) -> p c n", c=PACK)
            .unsqueeze(3)
            .to_broadcast([P, PACK, MODELS, ROWS]),
        )

        e_ps = psum.tile([P, PACK, P], F32)
        emb_w_by_t = emb_w_sb[:].rearrange("s (p t) -> s t p", t=PACK)
        for t in range(PACK):
            nc.tensor.matmul(
                out=e_ps[:, t, :],
                lhsT=emb_w_by_t[:, t, :],
                rhs=xT_sb[:].rearrange("s n i -> s (n i)"),
                start=True,
                stop=True,
            )
        e_grouped = keep.tile([P, P, PACK], BF16, align_bytes=64)
        e_codes = keep.tile([P, P], U32, align_bytes=64)
        e_scales = keep.tile([P, P], U8, align_bytes=64)

        b2_ps = psum.tile([P, PACK, P], BF16)
        for c in range(PACK):
            nc.tensor.transpose(
                b2_ps[:, c, :], b2T_wide[:, c, :, :].rearrange("p n i -> p (n i)"), ident[:]
            )
        b1T_ps = psum.tile([P, P], BF16, name="biasT_ps")
        nc.tensor.transpose(b1T_ps[:], b1_rows[:], ident[:])

        a_ps = [None] * 2
        a_sb = [None] * 2
        o_ps = [psum.tile([P, HALF], F32, name="o_ps_%d" % h) for h in range(2)]

        def quantise(c, cols):
            nc.vector.quantize_mx(
                out=w_codes[c][:, cols].bitcast(FP8X4),
                scales=w_scales[c][:, cols],
                in_=w_grouped[c][:, cols, :].rearrange("p w t -> p (w t)"),
            )

        def multiply(c, h):
            n = ORDER[c % MODELS]
            q = n % 2
            w = 1 - n // 2
            if c < MODELS:
                if c % 2 == 0 and h == 0:
                    a_ps[q] = psum_a.tile([P, 2, PACK, WINDOW], F32, name="a_ps")
                patches = slice((1 - w) * WINDOW, (2 - w) * WINDOW)
                for t in range(2 * h, 2 * h + 2):
                    nc.tensor.matmul_mx(
                        out=a_ps[q][:, w, t, :],
                        lhsT=w_codes[c][:, t * P : (t + 1) * P].bitcast(FP8X4),
                        lhsT_scale=w_scales[c][:, t * P : (t + 1) * P],
                        rhs=e_codes[:, patches].bitcast(FP8X4),
                        rhs_scale=e_scales[:, patches],
                        start=True,
                        stop=True,
                    )
            else:
                nc.tensor.matmul_mx(
                    out=o_ps[h][:],
                    lhsT=g_codes[:, q, w * P : (w + 1) * P].bitcast(FP8X4),
                    lhsT_scale=g_scales[:, q, w * P : (w + 1) * P],
                    rhs=w_codes[c][:, halves[h]].bitcast(FP8X4),
                    rhs_scale=w_scales[c][:, halves[h]],
                    start=(c == MODELS),
                    stop=(c == WEIGHTS - 1),
                )

        own = [slice(q * ROWS, (q + 1) * ROWS) for q in range(2)]
        b1T_sb = keep.tile([P, BIAS_ROWS], BF16)
        b1_by_pair = b1T_sb[:].rearrange("p (w q t) -> p q w t", w=2, q=2)

        def add_b1(q):
            a_sb[q] = work.tile([P, 2, ROWS, PACK], F32, name="a_sb")
            nc.vector.tensor_tensor(
                out=a_sb[q][:],
                in0=a_ps[q][:, :, :, own[q]].rearrange("p w t i -> p w i t"),
                in1=b1_by_pair[:, q].unsqueeze(2).to_broadcast([P, 2, ROWS, PACK]),
                op=ADD,
            )

        def gelu(q):
            nc.scalar.activation(out=g_window[:, q, :, own[q], :], in_=a_sb[q][:], func=GELU)

        def quantise_g(q):
            middle = slice(WINDOW, 3 * WINDOW)
            nc.vector.quantize_mx(
                out=g_codes[:, q, middle].bitcast(FP8X4),
                scales=g_scales[:, q, middle],
                in_=g_window[:, q].rearrange("p w j t -> p (w j t)"),
            )

        quantise(0, halves[0])
        quantise(0, halves[1])
        nc.vector.tensor_tensor(
            out=e_grouped[:],
            in0=e_ps[:].rearrange("p t r -> p r t"),
            in1=emb_b_sb[:].unsqueeze(1).to_broadcast([P, P, PACK]),
            op=ADD,
        )
        share_regrouping(1)
        nc.vector.quantize_mx(
            out=e_codes[:].bitcast(FP8X4),
            scales=e_scales[:],
            in_=e_grouped[:].rearrange("p r t -> p (r t)"),
        )
        multiply(0, 0)
        multiply(0, 1)

        for s in range(1, WEIGHTS):
            if s in (5, 7):
                quantise_g((s - 5) // 2)
            if s in (4, 6):
                gelu((s - 4) // 2)
            if 2 <= s < WEIGHTS - 1:
                quantise(s - 1, slice(0, WIDTH))
                multiply(s - 1, 0)
                multiply(s - 1, 1)
            if s in (3, 5):
                add_b1((s - 3) // 2)
            if s + 1 < WEIGHTS:
                share_regrouping(s + 1)
            if s == 1:
                nc.scalar.copy(out=b1T_sb[:], in_=b1T_ps[:, 0:BIAS_ROWS])

        for h in range(2):
            for c in range(WEIGHTS - 2, WEIGHTS):
                quantise(c, halves[h])
                multiply(c, h)

        b2_rows = keep.tile([P, WIDTH], BF16)
        nc.scalar.copy(out=b2_rows[:], in_=b2_ps[:].rearrange("p c f -> p (c f)"))

        o_sb = keep.tile([P, WIDTH], F32)
        out_rows = out.rearrange("n b c l f -> (n b c l) f")
        for h in range(2):
            nc.vector.tensor_tensor(
                out=o_sb[:, halves[h]], in0=o_ps[h][:], in1=b2_rows[:, halves[h]], op=ADD
            )
            nc.sync.dma_start(out=out_rows[:, halves[h]], in_=o_sb[:, halves[h]])
